import numpy as np
import ml_dtypes


def mxq(x, axis, fmt="e4m3"):
    dtype, down = {"e4m3": (ml_dtypes.float8_e4m3fn, 7), "e5m2": (ml_dtypes.float8_e5m2, 14)}[fmt]
    v = np.moveaxis(np.asarray(x, np.float32).astype(ml_dtypes.bfloat16).astype(np.float64), axis, -1)
    blocks = v.reshape(v.shape[:-1] + (-1, 32))
    amax = np.abs(blocks).max(-1, keepdims=True)
    byte = np.maximum(np.where(amax > 0, np.frexp(amax)[1] - 1 + 127, 0) - down, 1)
    scale = np.exp2(byte - 127.0)
    codes = (blocks / scale).astype(np.float32).astype(dtype).astype(np.float64)
    return np.moveaxis((codes * scale).reshape(v.shape), -1, axis)


WIDE = False


def mx_kscale(k):
    if not WIDE:
        return np.ones(k)
    levels = np.array([10, -10, 5, -5, 0])
    if k % 512:
        return np.exp2(np.random.permutation(np.resize(levels, k // 32))).repeat(32)
    a = np.empty((k // 512, 16))
    for p in range(k // 512):
        a[p, :8] = np.random.permutation(np.resize(levels, 8))
        for g in range(8):
            far = levels[np.abs(levels - a[p, g]) >= 10]
            a[p, g + 8] = far[np.random.randint(len(far))]
    return np.exp2(a.ravel()).repeat(32)


BF16 = ml_dtypes.bfloat16


def bf(x):
    return np.asarray(x, np.float32).astype(BF16)


def f64(x):
    return np.asarray(x).astype(np.float64)


B, S, D, H = 1, 4096, 2048, 2048


def setup_inputs():
    s, t = mx_kscale(D), mx_kscale(H)
    return {"audio_feature": bf(np.random.standard_normal((B, S, D)) * s),
            "W_phi": bf(np.random.standard_normal((D, H)) / np.sqrt(D) / s[:, None] * t),
            "b_phi": bf(np.random.standard_normal(H) * 0.2 * t),
            "W_theta": bf(np.random.standard_normal((D, H)) / np.sqrt(D) / s[:, None] / t),
            "b_theta": bf(np.random.standard_normal(H) * 0.2 / t)}


def reference(audio_feature, W_phi, b_phi, W_theta, b_theta):
    xq = mxq(f64(audio_feature), 2, "e4m3")
    phi_a = (xq @ mxq(f64(W_phi), 0, "e4m3")) + f64(b_phi)
    theta_a = (xq @ mxq(f64(W_theta), 0, "e4m3")) + f64(b_theta)
    scores = (mxq(phi_a, 2, "e4m3") @ mxq(theta_a, 2, "e4m3").transpose(0, 2, 1)) / np.sqrt(D)
    scores = np.maximum(scores, 0.0)
    return (scores + scores.transpose(0, 2, 1)) * 0.5

@@ -1,0 +1,306 @@
+from contextlib import ExitStack
+import math
+
+import concourse.mybir as mybir
+from concourse.masks import make_identity
+
+S, D, H = 4096, 2048, 2048
+FLOPS = 2 * S * D * H * 2 + 2 * S * S * H
+
+F32 = mybir.dt.float32
+BF16 = mybir.dt.bfloat16
+U32 = mybir.dt.uint32
+U8 = mybir.dt.uint8
+FP8X4 = mybir.dt.float8_e4m3fn_x4
+ACT = mybir.ActivationFunctionType
+ALU = mybir.AluOpType
+
+P = 128
+N_BLOCK = 21
+N_RAW = 6
+N_GROUPED = 3
+N_SMALL = 4
+N_PRAW = 2
+OUT_SCALE = 0.5 / math.sqrt(2048.0)
+
+
+def tile_selfattention_pa_l_kernel(tc, audio_feature, W_phi, b_phi, W_theta, b_theta, out):
+    nc = tc.nc
+    x_rows = audio_feature.flatten_outer_dims()
+    out_rows = out.flatten_outer_dims()
+    w_dram = (W_phi, W_theta)
+    b_dram = (b_phi, b_theta)
+
+    with ExitStack() as ctx:
+        sbuf = ctx.enter_context(tc.tile_pool(name="sbuf", bufs=1))
+        psum = ctx.enter_context(tc.psum_pool(name="psum", bufs=4))
+        ctx.enter_context(tc.manual_schedule())
+
+        def block_tile(name, shape, dtype):
+            return sbuf.tile(shape, dtype, name=name, tag="block", bufs=N_BLOCK, align_bytes=64)
+
+        def small_tile(name, shape, dtype):
+            return sbuf.tile(shape, dtype, name=name, tag="small", bufs=N_SMALL, align_bytes=64)
+
+        def acc_bank(name):
+            return psum.tile([P, 512], F32, name=name, tag="acc", bufs=4)
+
+        warm = sbuf.tile([P, 8], F32, name="warm")
+        nc.gpsimd.memset(warm[:], 0.0)
+        nc.scalar.activation(out=warm[:], in_=warm[:], func=ACT.Relu)
+        ident = sbuf.tile([P, P], F32, name="ident")
+        make_identity(nc, ident[:])
+        bias_bf = sbuf.tile([P, 2, 4, 4], BF16, name="bias_bf")
+        for which in range(2):
+            nc.scalar.dma_start(
+                out=bias_bf[:, which, :, :],
+                in_=b_dram[which].rearrange("(g p t) -> p g t", p=P, t=4),
+            )
+        bias = sbuf.tile([P, 32], F32, name="bias")
+
+        pending = []
+        loaded = {}
+        in_flight = [0]
+
+        def refill():
+            while pending and in_flight[0] < N_RAW:
+                kind, a, b = pending.pop(0)
+                if kind == "w":
+                    raw = sbuf.tile([P, 4, 512], BF16, name="w_raw", tag="raw", bufs=N_RAW, align_bytes=64)
+                    src = w_dram[a // 4][512 * b : 512 * (b + 1), 512 * (a % 4) : 512 * (a % 4 + 1)]
+                    nc.sync.dma_start(out=raw[:], in_=src.rearrange("(p j) c -> p j c", j=4))
+                else:
+                    raw = sbuf.tile([P, D], BF16, name="x_raw", tag="raw", bufs=N_RAW, align_bytes=64)
+                    nc.sync.dma_start(out=raw[:], in_=x_rows[P * a : P * (a + 1), :])
+                loaded[(kind, a, b)] = raw
+                in_flight[0] = in_flight[0] + 1
+
+        def take(kind, a, b):
+            raw = loaded.pop((kind, a, b))
+            in_flight[0] = in_flight[0] - 1
+            return raw
+
+        w_codes = {}
+        w_scales = {}
+
+        def w_copy(w, g):
+            raw = take("w", w, g)
+            grouped = sbuf.tile([P, 2048], BF16, name="w_grouped", tag="grouped", bufs=N_GROUPED, align_bytes=64)
+            nc.vector.tensor_copy(
+                out=grouped[:].rearrange("p (t m j) -> p t m j", t=4, j=4),
+                in_=raw[:].rearrange("p j (m t) -> p t m j", t=4),
+            )
+            refill()
+            return grouped
+
+        def w_quant(w, g, grouped):
+            if g == 0:
+                w_codes[w] = block_tile("w_codes", [P, 4, 512], U32)
+                w_scales[w] = sbuf.tile([P, 512], U8, name="w_scales", tag="w_scales", bufs=8, align_bytes=64)
+            nc.vector.quantize_mx(
+                out=w_codes[w][:, g, :].bitcast(FP8X4), scales=w_scales[w][4 * g : P, :], in_=grouped[:]
+            )
+
+        x_codes = {}
+        x_scales = {}
+
+        def x_turn(sc, pair):
+            rows = [take("x", 4 * sc + 2 * pair + r, 0) for r in range(2)]
+            made = []
+            for g in range(4):
+                bank = psum.tile([P, 2, 2, P], F32, name="x_bank", tag="turned", bufs=4)
+                for r in range(2):
+                    words = rows[r][:].bitcast(F32)
+                    for u in range(2):
+                        nc.tensor.transpose(bank[:, r, u, :], words[:, 256 * g + u : 256 * (g + 1) : 2], ident[:])
+                x_grouped = small_tile("x_grouped", [P, 1024], BF16)
+                nc.scalar.copy(
+                    out=x_grouped[:].bitcast(F32).rearrange("p (r k u) -> p r k u", r=2, u=2),
+                    in_=bank[:].rearrange("p r u k -> p r k u"),
+                )
+                made.append(x_grouped)
+            refill()
+            return made
+
+        def x_quant(sc, pair, made):
+            if pair == 0:
+                x_codes[sc] = block_tile("x_codes", [P, 4, 512], U32)
+                x_scales[sc] = sbuf.tile([P, 512], U8, name="x_scales", tag="x_scales", bufs=5, align_bytes=64)
+            cols = slice(256 * pair, 256 * (pair + 1))
+            for g in range(4):
+                nc.vector.quantize_mx(
+                    out=x_codes[sc][:, g, cols].bitcast(FP8X4), scales=x_scales[sc][4 * g : P, cols], in_=made[g][:]
+                )
+
+        pt_codes = {}
+        pt_scales = {}
+
+        def cell_group(w, sc, t, p_raw):
+            acc = acc_bank("acc1")
+            m_cols = slice(P * t, P * (t + 1))
+            for g in range(4):
+                nc.tensor.matmul_mx(
+                    out=acc[:],
+                    lhsT=w_codes[w][:, g, m_cols].bitcast(FP8X4),
+                    lhsT_scale=w_scales[w][4 * g : P, m_cols],
+                    rhs=x_codes[sc][:, g, :].bitcast(FP8X4),
+                    rhs_scale=x_scales[sc][4 * g : P, :],
+                    start=(g == 0),
+                    stop=(g == 3),
+                )
+            nc.scalar.activation(
+                out=p_raw[:, t, :], in_=acc[:], func=ACT.Identity, bias=bias[:, 4 * w + t : 4 * w + t + 1], scale=1.0
+            )
+
+        def p_copy(p_raw):
+            grouped = sbuf.tile([P, 2048], BF16, name="p_grouped", tag="grouped", bufs=N_GROUPED, align_bytes=64)
+            nc.vector.tensor_copy(
+                out=grouped[:].rearrange("p (n t) -> p n t", t=4), in_=p_raw[:].rearrange("p t n -> p n t")
+            )
+            return grouped
+
+        def p_quant(h, w, scl, grouped):
+            which, gh = w // 4, w % 4
+            if scl == 0:
+                pt_codes[(w, h)] = block_tile("pt_codes", [P, 2048], U32)
+                if gh == 0:
+                    pt_scales[(which, h)] = sbuf.tile(
+                        [P, 2048], U8, name="pt_scales", tag="pt_scales", bufs=4, align_bytes=64
+                    )
+            cols = slice(512 * scl, 512 * (scl + 1))
+            nc.vector.quantize_mx(
+                out=pt_codes[(w, h)][:, cols].bitcast(FP8X4),
+                scales=pt_scales[(which, h)][4 * gh : P, cols],
+                in_=grouped[:],
+            )
+
+        for g in range(4):
+            pending.append(("w", 0, g))
+        for rt in range(8):
+            pending.append(("x", rt, 0))
+        pending.append(("w", 1, 0))
+        pending.append(("w", 1, 1))
+        for rt in range(8, 12):
+            pending.append(("x", rt, 0))
+        pending.append(("w", 1, 2))
+        for rt in range(12, 16):
+            pending.append(("x", rt, 0))
+        for k in range(7, 32):
+            pending.append(("w", k // 4, k % 4))
+        for rt in range(16, 32):
+            pending.append(("x", rt, 0))
+        refill()
+
+        nc.vector.tensor_copy(out=bias[:], in_=bias_bf[:].rearrange("p a g t -> p (a g t)"))
+        g0 = w_copy(0, 0)
+        g1 = w_copy(0, 1)
+        w_quant(0, 0, g0)
+        g2 = w_copy(0, 2)
+        w_quant(0, 1, g1)
+        g3 = w_copy(0, 3)
+        w_quant(0, 2, g2)
+        first_a = x_turn(0, 0)
+        w_quant(0, 3, g3)
+        x_quant(0, 0, first_a)
+        x_quant(0, 1, x_turn(0, 1))
+        g4 = w_copy(1, 0)
+        late = [(1, 0, g4)]
+        waiting = []
+
+        for n in range(64):
+            h, w, scl = n // 32, (n % 32) // 4, n % 4
+            sc = 4 * h + scl
+            k = n + 5
+            fresh = None
+            if k < 32:
+                fresh = (k // 4, k % 4, w_copy(k // 4, k % 4))
+            if late:
+                lw, lg, lgrouped = late.pop(0)
+                w_quant(lw, lg, lgrouped)
+            if waiting:
+                qh, qw, qscl, qg = waiting.pop(0)
+                p_quant(qh, qw, qscl, qg)
+            turn = None
+            if n < 3:
+                turn = n + 1
+            if 28 <= n < 32:
+                turn = n - 24
+            p_raw = sbuf.tile([P, 4, 512], BF16, name="p_raw", tag="p_raw", bufs=N_PRAW, align_bytes=64)
+            cell_group(w, sc, 0, p_raw)
+            if turn is not None:
+                x_quant(turn, 0, x_turn(turn, 0))
+            cell_group(w, sc, 1, p_raw)
+            if turn is not None:
+                x_quant(turn, 1, x_turn(turn, 1))
+            cell_group(w, sc, 2, p_raw)
+            cell_group(w, sc, 3, p_raw)
+            waiting.append((h, w, scl, p_copy(p_raw)))
+            if fresh is not None:
+                w_quant(fresh[0], fresh[1], fresh[2])
+
+        def score_group(name, a_which, a_tok, b_which, b_tok):
+            acc = acc_bank(name)
+            ah, ac = a_tok // 2048, a_tok % 2048
+            bh, bc = b_tok // 2048, b_tok % 2048
+            for g in range(4):
+                nc.tensor.matmul_mx(
+                    out=acc[:],
+                    lhsT=pt_codes[(4 * a_which + g, ah)][:, ac : ac + P].bitcast(FP8X4),
+                    lhsT_scale=pt_scales[(a_which, ah)][4 * g : P, ac : ac + P],
+                    rhs=pt_codes[(4 * b_which + g, bh)][:, bc : bc + 512].bitcast(FP8X4),
+                    rhs_scale=pt_scales[(b_which, bh)][4 * g : P, bc : bc + 512],
+                    start=(g == 0),
+                    stop=(g == 3),
+                )
+            return acc
+
+        def mirror(ib, jb, o_all):
+            e_all = block_tile("e_all", [P, 4, 512], F32)
+            for j in range(4):
+                bank = psum.tile([P, 4, P], F32, name="o_bank", tag="turned", bufs=4)
+                for i in range(4):
+                    nc.tensor.transpose(bank[:, i, :], o_all[:, i, P * j : P * (j + 1)], ident[:])
+                flat = bank[:].rearrange("p i q -> p (i q)")
+                if ib == jb:
+                    nc.vector.tensor_tensor(out=e_all[:, j, :], in0=flat, in1=o_all[:, j, :], op=ALU.add)
+                else:
+                    nc.vector.tensor_copy(out=e_all[:, j, :], in_=flat)
+            nc.sync.dma_start(
+                out=out_rows[512 * jb : 512 * (jb + 1), 512 * ib : 512 * (ib + 1)].rearrange("(j p) c -> p j c", p=P),
+                in_=e_all[:],
+            )
+
+        owed = []
+        for jb in range(8):
+            for ib in range(jb + 1):
+                o_all = block_tile("o_all", [P, 4, 512], F32)
+                passes = 0
+                for i in range(4):
+                    tok = 512 * ib + P * i
+                    acc_a = score_group("acc_a", 0, tok, 1, 512 * jb)
+                    passes += 4
+                    if ib == jb:
+                        nc.scalar.activation(out=o_all[:, i, :], in_=acc_a[:], func=ACT.Relu, scale=OUT_SCALE)
+                    else:
+                        acc_b = score_group("acc_b", 1, tok, 0, 512 * jb)
+                        passes += 4
+                        half = small_tile("half", [P, 512], F32)
+                        nc.scalar.activation(out=half[:], in_=acc_a[:], func=ACT.Relu, scale=OUT_SCALE)
+                        nc.scalar.activation(out=o_all[:, i, :], in_=acc_b[:], func=ACT.Relu, scale=OUT_SCALE)
+                        nc.vector.tensor_tensor(out=o_all[:, i, :], in0=o_all[:, i, :], in1=half[:], op=ALU.add)
+                    if waiting:
+                        qh, qw, qscl, qg = waiting.pop(0)
+                        p_quant(qh, qw, qscl, qg)
+                    if owed and passes >= 8:
+                        oi, oj, oo = owed.pop(0)
+                        mirror(oi, oj, oo)
+                if ib != jb:
+                    nc.sync.dma_start(
+                        out=out_rows[512 * ib : 512 * (ib + 1), 512 * jb : 512 * (jb + 1)].rearrange(
+                            "(i p) c -> p i c", p=P
+                        ),
+                        in_=o_all[:],
+                    )
+                owed.append((ib, jb, o_all))
+        oi, oj, oo = owed.pop(0)
+        mirror(oi, oj, oo)

@@ -21,6 +21,7 @@ N_RAW = 6
 N_GROUPED = 3
 N_SMALL = 4
 N_PRAW = 2
+MIRROR_GROUP = 3
 OUT_SCALE = 0.5 / math.sqrt(2048.0)
 
 
@@ -62,8 +63,12 @@ def tile_selfattention_pa_l_kernel(tc, audio_feature, W_phi, b_phi, W_theta, b_t
         loaded = {}
         in_flight = [0]
 
+        def room():
+            kind, a, b = pending[0]
+            return N_RAW - 2 if (kind == "x" and a >= 16) else N_RAW
+
         def refill():
-            while pending and in_flight[0] < N_RAW:
+            while pending and in_flight[0] < room():
                 kind, a, b = pending.pop(0)
                 if kind == "w":
                     raw = sbuf.tile([P, 4, 512], BF16, name="w_raw", tag="raw", bufs=N_RAW, align_bytes=64)
@@ -104,20 +109,42 @@ def tile_selfattention_pa_l_kernel(tc, audio_feature, W_phi, b_phi, W_theta, b_t
         x_codes = {}
         x_scales = {}
 
-        def x_turn(sc, pair):
-            rows = [take("x", 4 * sc + 2 * pair + r, 0) for r in range(2)]
+        def x_sort(sc, pair):
+            ordered = []
+            for r in range(2):
+                row = take("x", 4 * sc + 2 * pair + r, 0)
+                x_sorted = sbuf.tile([P, 1024], F32, name="x_sorted", tag="raw", bufs=N_RAW, align_bytes=64)
+                nc.scalar.copy(
+                    out=x_sorted[:].rearrange("p (g u k) -> p g u k", g=4, u=2),
+                    in_=row[:].bitcast(F32).rearrange("p (g k u) -> p g u k", g=4, u=2),
+                )
+                ordered.append(x_sorted)
+            refill()
+            return ordered
+
+        def x_turn(sc, pair, ordered):
+            sort_first = ordered is not None
+            rows = None
+            if not sort_first:
+                rows = [take("x", 4 * sc + 2 * pair + r, 0) for r in range(2)]
             made = []
             for g in range(4):
                 bank = psum.tile([P, 2, 2, P], F32, name="x_bank", tag="turned", bufs=4)
                 for r in range(2):
-                    words = rows[r][:].bitcast(F32)
                     for u in range(2):
-                        nc.tensor.transpose(bank[:, r, u, :], words[:, 256 * g + u : 256 * (g + 1) : 2], ident[:])
+                        if sort_first:
+                            first = 256 * g + P * u
+                            nc.tensor.transpose(bank[:, r, u, :], ordered[r][:, first : first + P], ident[:])
+                        else:
+                            words = rows[r][:].bitcast(F32)
+                            nc.tensor.transpose(bank[:, r, u, :], words[:, 256 * g + u : 256 * (g + 1) : 2], ident[:])
                 x_grouped = small_tile("x_grouped", [P, 1024], BF16)
-                nc.scalar.copy(
-                    out=x_grouped[:].bitcast(F32).rearrange("p (r k u) -> p r k u", r=2, u=2),
-                    in_=bank[:].rearrange("p r u k -> p r k u"),
-                )
+                dst = x_grouped[:].bitcast(F32).rearrange("p (r k u) -> p r k u", r=2, u=2)
+                src = bank[:].rearrange("p r u k -> p r k u")
+                if sort_first and g % 2 == 1:
+                    nc.vector.tensor_copy(out=dst, in_=src)
+                else:
+                    nc.scalar.copy(out=dst, in_=src)
                 made.append(x_grouped)
             refill()
             return made
@@ -199,13 +226,14 @@ def tile_selfattention_pa_l_kernel(tc, audio_feature, W_phi, b_phi, W_theta, b_t
         w_quant(0, 1, g1)
         g3 = w_copy(0, 3)
         w_quant(0, 2, g2)
-        first_a = x_turn(0, 0)
+        first_a = x_turn(0, 0, None)
         w_quant(0, 3, g3)
         x_quant(0, 0, first_a)
-        x_quant(0, 1, x_turn(0, 1))
+        x_quant(0, 1, x_turn(0, 1, None))
         g4 = w_copy(1, 0)
         late = [(1, 0, g4)]
         waiting = []
+        sorted_rows = []
 
         for n in range(64):
             h, w, scl = n // 32, (n % 32) // 4, n % 4
@@ -220,18 +248,17 @@ def tile_selfattention_pa_l_kernel(tc, audio_feature, W_phi, b_phi, W_theta, b_t
             if waiting:
                 qh, qw, qscl, qg = waiting.pop(0)
                 p_quant(qh, qw, qscl, qg)
-            turn = None
-            if n < 3:
-                turn = n + 1
-            if 28 <= n < 32:
-                turn = n - 24
             p_raw = sbuf.tile([P, 4, 512], BF16, name="p_raw", tag="p_raw", bufs=N_PRAW, align_bytes=64)
             cell_group(w, sc, 0, p_raw)
-            if turn is not None:
-                x_quant(turn, 0, x_turn(turn, 0))
+            if n < 3:
+                x_quant(n + 1, 0, x_turn(n + 1, 0, None))
+            if 27 <= n < 35:
+                x_quant(4 + (n - 27) // 2, (n - 27) % 2, x_turn(4 + (n - 27) // 2, (n - 27) % 2, sorted_rows.pop(0)))
             cell_group(w, sc, 1, p_raw)
-            if turn is not None:
-                x_quant(turn, 1, x_turn(turn, 1))
+            if n < 3:
+                x_quant(n + 1, 1, x_turn(n + 1, 1, None))
+            if 26 <= n < 34:
+                sorted_rows.append(x_sort(4 + (n - 26) // 2, (n - 26) % 2))
             cell_group(w, sc, 2, p_raw)
             cell_group(w, sc, 3, p_raw)
             waiting.append((h, w, scl, p_copy(p_raw)))
@@ -254,53 +281,68 @@ def tile_selfattention_pa_l_kernel(tc, audio_feature, W_phi, b_phi, W_theta, b_t
                 )
             return acc
 
-        def mirror(ib, jb, o_all):
-            e_all = block_tile("e_all", [P, 4, 512], F32)
-            for j in range(4):
-                bank = psum.tile([P, 4, P], F32, name="o_bank", tag="turned", bufs=4)
-                for i in range(4):
-                    nc.tensor.transpose(bank[:, i, :], o_all[:, i, P * j : P * (j + 1)], ident[:])
-                flat = bank[:].rearrange("p i q -> p (i q)")
-                if ib == jb:
-                    nc.vector.tensor_tensor(out=e_all[:, j, :], in0=flat, in1=o_all[:, j, :], op=ALU.add)
-                else:
-                    nc.vector.tensor_copy(out=e_all[:, j, :], in_=flat)
-            nc.sync.dma_start(
-                out=out_rows[512 * jb : 512 * (jb + 1), 512 * ib : 512 * (ib + 1)].rearrange("(j p) c -> p j c", p=P),
-                in_=e_all[:],
-            )
+        def mirror(group, fine):
+            turn_of = [0]
+            for ib, jb, o_all in group:
+                for jp in range(2):
+                    e_half = sbuf.tile([P, 2, 512], F32, name="e_half", tag="raw", bufs=N_RAW, align_bytes=64)
+                    for jj in range(2):
+                        j = 2 * jp + jj
+                        bank = psum.tile([P, 4, P], F32, name="o_bank", tag="turned", bufs=4)
+                        for i in range(4):
+                            nc.tensor.transpose(bank[:, i, :], o_all[:, i, P * j : P * (j + 1)], ident[:])
+                        flat = bank[:].rearrange("p i q -> p (i q)")
+                        if ib == jb:
+                            nc.vector.tensor_tensor(out=e_half[:, jj, :], in0=flat, in1=o_all[:, j, :], op=ALU.add)
+                        elif turn_of[0] % 2 == 0:
+                            nc.vector.tensor_copy(out=e_half[:, jj, :], in_=flat)
+                        else:
+                            nc.scalar.copy(out=e_half[:, jj, :], in_=flat)
+                        turn_of[0] = turn_of[0] + 1
+                        if fine:
+                            r0 = 512 * jb + P * j
+                            nc.sync.dma_start(
+                                out=out_rows[r0 : r0 + P, 512 * ib : 512 * (ib + 1)], in_=e_half[:, jj, :]
+                            )
+                    if not fine:
+                        r0 = 512 * jb + 256 * jp
+                        nc.sync.dma_start(
+                            out=out_rows[r0 : r0 + 256, 512 * ib : 512 * (ib + 1)].rearrange("(j p) c -> p j c", p=P),
+                            in_=e_half[:],
+                        )
 
+        blocks = [(ib, jb) for jb in range(8) for ib in range(jb + 1)]
         owed = []
-        for jb in range(8):
-            for ib in range(jb + 1):
-                o_all = block_tile("o_all", [P, 4, 512], F32)
-                passes = 0
-                for i in range(4):
-                    tok = 512 * ib + P * i
-                    acc_a = score_group("acc_a", 0, tok, 1, 512 * jb)
-                    passes += 4
-                    if ib == jb:
-                        nc.scalar.activation(out=o_all[:, i, :], in_=acc_a[:], func=ACT.Relu, scale=OUT_SCALE)
-                    else:
-                        acc_b = score_group("acc_b", 1, tok, 0, 512 * jb)
-                        passes += 4
-                        half = small_tile("half", [P, 512], F32)
-                        nc.scalar.activation(out=half[:], in_=acc_a[:], func=ACT.Relu, scale=OUT_SCALE)
-                        nc.scalar.activation(out=o_all[:, i, :], in_=acc_b[:], func=ACT.Relu, scale=OUT_SCALE)
-                        nc.vector.tensor_tensor(out=o_all[:, i, :], in0=o_all[:, i, :], in1=half[:], op=ALU.add)
-                    if waiting:
-                        qh, qw, qscl, qg = waiting.pop(0)
-                        p_quant(qh, qw, qscl, qg)
-                    if owed and passes >= 8:
-                        oi, oj, oo = owed.pop(0)
-                        mirror(oi, oj, oo)
+        for n, (ib, jb) in enumerate(blocks):
+            o_all = block_tile("o_all", [P, 4, 512], F32)
+            passes = 0
+            for i in range(4):
+                tok = 512 * ib + P * i
+                acc_a = score_group("acc_a", 0, tok, 1, 512 * jb)
+                passes += 4
+                acc_b = None
                 if ib != jb:
-                    nc.sync.dma_start(
-                        out=out_rows[512 * ib : 512 * (ib + 1), 512 * jb : 512 * (jb + 1)].rearrange(
-                            "(i p) c -> p i c", p=P
-                        ),
-                        in_=o_all[:],
-                    )
-                owed.append((ib, jb, o_all))
-        oi, oj, oo = owed.pop(0)
-        mirror(oi, oj, oo)
+                    acc_b = score_group("acc_b", 1, tok, 0, 512 * jb)
+                    passes += 4
+                if passes == 8 and (len(owed) == MIRROR_GROUP or (owed and n == len(blocks) - 1)):
+                    mirror(owed, False)
+                    owed = []
+                if ib == jb:
+                    nc.scalar.activation(out=o_all[:, i, :], in_=acc_a[:], func=ACT.Relu, scale=OUT_SCALE)
+                else:
+                    half = small_tile("half", [P, 512], F32)
+                    nc.scalar.activation(out=half[:], in_=acc_a[:], func=ACT.Relu, scale=OUT_SCALE)
+                    nc.scalar.activation(out=o_all[:, i, :], in_=acc_b[:], func=ACT.Relu, scale=OUT_SCALE)
+                    nc.vector.tensor_tensor(out=o_all[:, i, :], in0=o_all[:, i, :], in1=half[:], op=ALU.add)
+                if waiting:
+                    qh, qw, qscl, qg = waiting.pop(0)
+                    p_quant(qh, qw, qscl, qg)
+            if ib != jb:
+                nc.sync.dma_start(
+                    out=out_rows[512 * ib : 512 * (ib + 1), 512 * jb : 512 * (jb + 1)].rearrange(
+                        "(i p) c -> p i c", p=P
+                    ),
+                    in_=o_all[:],
+                )
+            owed.append((ib, jb, o_all))
+        mirror(owed, True)

@@ -21,7 +21,6 @@ N_RAW = 6
 N_GROUPED = 3
 N_SMALL = 4
 N_PRAW = 2
-MIRROR_GROUP = 3
 OUT_SCALE = 0.5 / math.sqrt(2048.0)
 
 
@@ -281,68 +280,59 @@ def tile_selfattention_pa_l_kernel(tc, audio_feature, W_phi, b_phi, W_theta, b_t
                 )
             return acc
 
-        def mirror(group, fine):
-            turn_of = [0]
-            for ib, jb, o_all in group:
-                for jp in range(2):
-                    e_half = sbuf.tile([P, 2, 512], F32, name="e_half", tag="raw", bufs=N_RAW, align_bytes=64)
-                    for jj in range(2):
-                        j = 2 * jp + jj
-                        bank = psum.tile([P, 4, P], F32, name="o_bank", tag="turned", bufs=4)
-                        for i in range(4):
-                            nc.tensor.transpose(bank[:, i, :], o_all[:, i, P * j : P * (j + 1)], ident[:])
-                        flat = bank[:].rearrange("p i q -> p (i q)")
-                        if ib == jb:
-                            nc.vector.tensor_tensor(out=e_half[:, jj, :], in0=flat, in1=o_all[:, j, :], op=ALU.add)
-                        elif turn_of[0] % 2 == 0:
-                            nc.vector.tensor_copy(out=e_half[:, jj, :], in_=flat)
-                        else:
-                            nc.scalar.copy(out=e_half[:, jj, :], in_=flat)
-                        turn_of[0] = turn_of[0] + 1
-                        if fine:
-                            r0 = 512 * jb + P * j
-                            nc.sync.dma_start(
-                                out=out_rows[r0 : r0 + P, 512 * ib : 512 * (ib + 1)], in_=e_half[:, jj, :]
-                            )
-                    if not fine:
-                        r0 = 512 * jb + 256 * jp
-                        nc.sync.dma_start(
-                            out=out_rows[r0 : r0 + 256, 512 * ib : 512 * (ib + 1)].rearrange("(j p) c -> p j c", p=P),
-                            in_=e_half[:],
-                        )
-
-        blocks = [(ib, jb) for jb in range(8) for ib in range(jb + 1)]
-        owed = []
-        for n, (ib, jb) in enumerate(blocks):
-            o_all = block_tile("o_all", [P, 4, 512], F32)
-            passes = 0
-            for i in range(4):
-                tok = 512 * ib + P * i
-                acc_a = score_group("acc_a", 0, tok, 1, 512 * jb)
-                passes += 4
-                acc_b = None
-                if ib != jb:
-                    acc_b = score_group("acc_b", 1, tok, 0, 512 * jb)
-                    passes += 4
-                if passes == 8 and (len(owed) == MIRROR_GROUP or (owed and n == len(blocks) - 1)):
-                    mirror(owed, False)
-                    owed = []
+        def mirror(ib, jb, o_all, fine):
+            e_all = block_tile("e_all", [P, 4, 512], F32)
+            for j in range(4):
+                bank = psum.tile([P, 4, P], F32, name="o_bank", tag="turned", bufs=4)
+                for i in range(4):
+                    nc.tensor.transpose(bank[:, i, :], o_all[:, i, P * j : P * (j + 1)], ident[:])
+                flat = bank[:].rearrange("p i q -> p (i q)")
                 if ib == jb:
-                    nc.scalar.activation(out=o_all[:, i, :], in_=acc_a[:], func=ACT.Relu, scale=OUT_SCALE)
+                    nc.vector.tensor_tensor(out=e_all[:, j, :], in0=flat, in1=o_all[:, j, :], op=ALU.add)
                 else:
-                    half = small_tile("half", [P, 512], F32)
-                    nc.scalar.activation(out=half[:], in_=acc_a[:], func=ACT.Relu, scale=OUT_SCALE)
-                    nc.scalar.activation(out=o_all[:, i, :], in_=acc_b[:], func=ACT.Relu, scale=OUT_SCALE)
-                    nc.vector.tensor_tensor(out=o_all[:, i, :], in0=o_all[:, i, :], in1=half[:], op=ALU.add)
-                if waiting:
-                    qh, qw, qscl, qg = waiting.pop(0)
-                    p_quant(qh, qw, qscl, qg)
-            if ib != jb:
+                    nc.vector.tensor_copy(out=e_all[:, j, :], in_=flat)
+                if fine:
+                    r0 = 512 * jb + P * j
+                    nc.sync.dma_start(out=out_rows[r0 : r0 + P, 512 * ib : 512 * (ib + 1)], in_=e_all[:, j, :])
+            if not fine:
                 nc.sync.dma_start(
-                    out=out_rows[512 * ib : 512 * (ib + 1), 512 * jb : 512 * (jb + 1)].rearrange(
-                        "(i p) c -> p i c", p=P
+                    out=out_rows[512 * jb : 512 * (jb + 1), 512 * ib : 512 * (ib + 1)].rearrange(
+                        "(j p) c -> p j c", p=P
                     ),
-                    in_=o_all[:],
+                    in_=e_all[:],
                 )
-            owed.append((ib, jb, o_all))
-        mirror(owed, True)
+
+        owed = []
+        for jb in range(8):
+            for ib in range(jb + 1):
+                o_all = block_tile("o_all", [P, 4, 512], F32)
+                passes = 0
+                for i in range(4):
+                    tok = 512 * ib + P * i
+                    acc_a = score_group("acc_a", 0, tok, 1, 512 * jb)
+                    passes += 4
+                    if ib == jb:
+                        nc.scalar.activation(out=o_all[:, i, :], in_=acc_a[:], func=ACT.Relu, scale=OUT_SCALE)
+                    else:
+                        acc_b = score_group("acc_b", 1, tok, 0, 512 * jb)
+                        passes += 4
+                        half = small_tile("half", [P, 512], F32)
+                        nc.scalar.activation(out=half[:], in_=acc_a[:], func=ACT.Relu, scale=OUT_SCALE)
+                        nc.scalar.activation(out=o_all[:, i, :], in_=acc_b[:], func=ACT.Relu, scale=OUT_SCALE)
+                        nc.vector.tensor_tensor(out=o_all[:, i, :], in0=o_all[:, i, :], in1=half[:], op=ALU.add)
+                    if waiting:
+                        qh, qw, qscl, qg = waiting.pop(0)
+                        p_quant(qh, qw, qscl, qg)
+                    if owed and passes >= 8:
+                        oi, oj, oo = owed.pop(0)
+                        mirror(oi, oj, oo, False)
+                if ib != jb:
+                    nc.sync.dma_start(
+                        out=out_rows[512 * ib : 512 * (ib + 1), 512 * jb : 512 * (jb + 1)].rearrange(
+                            "(i p) c -> p i c", p=P
+                        ),
+                        in_=o_all[:],
+                    )
+                owed.append((ib, jb, o_all))
+        oi, oj, oo = owed.pop(0)
+        mirror(oi, oj, oo, True)

from contextlib import ExitStack
import math

import concourse.mybir as mybir
from concourse.masks import make_identity

S, D, H = 4096, 2048, 2048
FLOPS = 2 * S * D * H * 2 + 2 * S * S * H

F32 = mybir.dt.float32
BF16 = mybir.dt.bfloat16
U32 = mybir.dt.uint32
U8 = mybir.dt.uint8
FP8X4 = mybir.dt.float8_e4m3fn_x4
ACT = mybir.ActivationFunctionType
ALU = mybir.AluOpType

P = 128
N_BLOCK = 21
N_RAW = 6
N_GROUPED = 3
N_SMALL = 4
N_PRAW = 2
OUT_SCALE = 0.5 / math.sqrt(2048.0)


def tile_selfattention_pa_l_kernel(tc, audio_feature, W_phi, b_phi, W_theta, b_theta, out):
    nc = tc.nc
    x_rows = audio_feature.flatten_outer_dims()
    out_rows = out.flatten_outer_dims()
    w_dram = (W_phi, W_theta)
    b_dram = (b_phi, b_theta)

    with ExitStack() as ctx:
        sbuf = ctx.enter_context(tc.tile_pool(name="sbuf", bufs=1))
        psum = ctx.enter_context(tc.psum_pool(name="psum", bufs=4))
        ctx.enter_context(tc.manual_schedule())

        def block_tile(name, shape, dtype):
            return sbuf.tile(shape, dtype, name=name, tag="block", bufs=N_BLOCK, align_bytes=64)

        def small_tile(name, shape, dtype):
            return sbuf.tile(shape, dtype, name=name, tag="small", bufs=N_SMALL, align_bytes=64)

        def acc_bank(name):
            return psum.tile([P, 512], F32, name=name, tag="acc", bufs=4)

        warm = sbuf.tile([P, 8], F32, name="warm")
        nc.gpsimd.memset(warm[:], 0.0)
        nc.scalar.activation(out=warm[:], in_=warm[:], func=ACT.Relu)
        ident = sbuf.tile([P, P], F32, name="ident")
        make_identity(nc, ident[:])
        bias_bf = sbuf.tile([P, 2, 4, 4], BF16, name="bias_bf")
        for which in range(2):
            nc.scalar.dma_start(
                out=bias_bf[:, which, :, :],
                in_=b_dram[which].rearrange("(g p t) -> p g t", p=P, t=4),
            )
        bias = sbuf.tile([P, 32], F32, name="bias")

        pending = []
        loaded = {}
        in_flight = [0]

        def room():
            kind, a, b = pending[0]
            return N_RAW - 2 if (kind == "x" and a >= 16) else N_RAW

        def refill():
            while pending and in_flight[0] < room():
                kind, a, b = pending.pop(0)
                if kind == "w":
                    raw = sbuf.tile([P, 4, 512], BF16, name="w_raw", tag="raw", bufs=N_RAW, align_bytes=64)
                    src = w_dram[a // 4][512 * b : 512 * (b + 1), 512 * (a % 4) : 512 * (a % 4 + 1)]
                    nc.sync.dma_start(out=raw[:], in_=src.rearrange("(p j) c -> p j c", j=4))
                else:
                    raw = sbuf.tile([P, D], BF16, name="x_raw", tag="raw", bufs=N_RAW, align_bytes=64)
                    nc.sync.dma_start(out=raw[:], in_=x_rows[P * a : P * (a + 1), :])
                loaded[(kind, a, b)] = raw
                in_flight[0] = in_flight[0] + 1

        def take(kind, a, b):
            raw = loaded.pop((kind, a, b))
            in_flight[0] = in_flight[0] - 1
            return raw

        w_codes = {}
        w_scales = {}

        def w_copy(w, g):
            raw = take("w", w, g)
            grouped = sbuf.tile([P, 2048], BF16, name="w_grouped", tag="grouped", bufs=N_GROUPED, align_bytes=64)
            nc.vector.tensor_copy(
                out=grouped[:].rearrange("p (t m j) -> p t m j", t=4, j=4),
                in_=raw[:].rearrange("p j (m t) -> p t m j", t=4),
            )
            refill()
            return grouped

        def w_quant(w, g, grouped):
            if g == 0:
                w_codes[w] = block_tile("w_codes", [P, 4, 512], U32)
                w_scales[w] = sbuf.tile([P, 512], U8, name="w_scales", tag="w_scales", bufs=8, align_bytes=64)
            nc.vector.quantize_mx(
                out=w_codes[w][:, g, :].bitcast(FP8X4), scales=w_scales[w][4 * g : P, :], in_=grouped[:]
            )

        x_codes = {}
        x_scales = {}

        def x_sort(sc, pair):
            ordered = []
            for r in range(2):
                row = take("x", 4 * sc + 2 * pair + r, 0)
                x_sorted = sbuf.tile([P, 1024], F32, name="x_sorted", tag="raw", bufs=N_RAW, align_bytes=64)
                nc.scalar.copy(
                    out=x_sorted[:].rearrange("p (g u k) -> p g u k", g=4, u=2),
                    in_=row[:].bitcast(F32).rearrange("p (g k u) -> p g u k", g=4, u=2),
                )
                ordered.append(x_sorted)
            refill()
            return ordered

        def x_turn(sc, pair, ordered):
            sort_first = ordered is not None
            rows = None
            if not sort_first:
                rows = [take("x", 4 * sc + 2 * pair + r, 0) for r in range(2)]
            made = []
            for g in range(4):
                bank = psum.tile([P, 2, 2, P], F32, name="x_bank", tag="turned", bufs=4)
                for r in range(2):
                    for u in range(2):
                        if sort_first:
                            first = 256 * g + P * u
                            nc.tensor.transpose(bank[:, r, u, :], ordered[r][:, first : first + P], ident[:])
                        else:
                            words = rows[r][:].bitcast(F32)
                            nc.tensor.transpose(bank[:, r, u, :], words[:, 256 * g + u : 256 * (g + 1) : 2], ident[:])
                x_grouped = small_tile("x_grouped", [P, 1024], BF16)
                dst = x_grouped[:].bitcast(F32).rearrange("p (r k u) -> p r k u", r=2, u=2)
                src = bank[:].rearrange("p r u k -> p r k u")
                if sort_first and g % 2 == 1:
                    nc.vector.tensor_copy(out=dst, in_=src)
                else:
                    nc.scalar.copy(out=dst, in_=src)
                made.append(x_grouped)
            refill()
            return made

        def x_quant(sc, pair, made):
            if pair == 0:
                x_codes[sc] = block_tile("x_codes", [P, 4, 512], U32)
                x_scales[sc] = sbuf.tile([P, 512], U8, name="x_scales", tag="x_scales", bufs=5, align_bytes=64)
            cols = slice(256 * pair, 256 * (pair + 1))
            for g in range(4):
                nc.vector.quantize_mx(
                    out=x_codes[sc][:, g, cols].bitcast(FP8X4), scales=x_scales[sc][4 * g : P, cols], in_=made[g][:]
                )

        pt_codes = {}
        pt_scales = {}

        def cell_group(w, sc, t, p_raw):
            acc = acc_bank("acc1")
            m_cols = slice(P * t, P * (t + 1))
            for g in range(4):
                nc.tensor.matmul_mx(
                    out=acc[:],
                    lhsT=w_codes[w][:, g, m_cols].bitcast(FP8X4),
                    lhsT_scale=w_scales[w][4 * g : P, m_cols],
                    rhs=x_codes[sc][:, g, :].bitcast(FP8X4),
                    rhs_scale=x_scales[sc][4 * g : P, :],
                    start=(g == 0),
                    stop=(g == 3),
                )
            nc.scalar.activation(
                out=p_raw[:, t, :], in_=acc[:], func=ACT.Identity, bias=bias[:, 4 * w + t : 4 * w + t + 1], scale=1.0
            )

        def p_copy(p_raw):
            grouped = sbuf.tile([P, 2048], BF16, name="p_grouped", tag="grouped", bufs=N_GROUPED, align_bytes=64)
            nc.vector.tensor_copy(
                out=grouped[:].rearrange("p (n t) -> p n t", t=4), in_=p_raw[:].rearrange("p t n -> p n t")
            )
            return grouped

        def p_quant(h, w, scl, grouped):
            which, gh = w // 4, w % 4
            if scl == 0:
                pt_codes[(w, h)] = block_tile("pt_codes", [P, 2048], U32)
                if gh == 0:
                    pt_scales[(which, h)] = sbuf.tile(
                        [P, 2048], U8, name="pt_scales", tag="pt_scales", bufs=4, align_bytes=64
                    )
            cols = slice(512 * scl, 512 * (scl + 1))
            nc.vector.quantize_mx(
                out=pt_codes[(w, h)][:, cols].bitcast(FP8X4),
                scales=pt_scales[(which, h)][4 * gh : P, cols],
                in_=grouped[:],
            )

        for g in range(4):
            pending.append(("w", 0, g))
        for rt in range(8):
            pending.append(("x", rt, 0))
        pending.append(("w", 1, 0))
        pending.append(("w", 1, 1))
        for rt in range(8, 12):
            pending.append(("x", rt, 0))
        pending.append(("w", 1, 2))
        for rt in range(12, 16):
            pending.append(("x", rt, 0))
        for k in range(7, 32):
            pending.append(("w", k // 4, k % 4))
        for rt in range(16, 32):
            pending.append(("x", rt, 0))
        refill()

        nc.vector.tensor_copy(out=bias[:], in_=bias_bf[:].rearrange("p a g t -> p (a g t)"))
        g0 = w_copy(0, 0)
        g1 = w_copy(0, 1)
        w_quant(0, 0, g0)
        g2 = w_copy(0, 2)
        w_quant(0, 1, g1)
        g3 = w_copy(0, 3)
        w_quant(0, 2, g2)
        first_a = x_turn(0, 0, None)
        w_quant(0, 3, g3)
        x_quant(0, 0, first_a)
        x_quant(0, 1, x_turn(0, 1, None))
        g4 = w_copy(1, 0)
        late = [(1, 0, g4)]
        waiting = []
        sorted_rows = []

        for n in range(64):
            h, w, scl = n // 32, (n % 32) // 4, n % 4
            sc = 4 * h + scl
            k = n + 5
            fresh = None
            if k < 32:
                fresh = (k // 4, k % 4, w_copy(k // 4, k % 4))
            if late:
                lw, lg, lgrouped = late.pop(0)
                w_quant(lw, lg, lgrouped)
            if waiting:
                qh, qw, qscl, qg = waiting.pop(0)
                p_quant(qh, qw, qscl, qg)
            p_raw = sbuf.tile([P, 4, 512], BF16, name="p_raw", tag="p_raw", bufs=N_PRAW, align_bytes=64)
            cell_group(w, sc, 0, p_raw)
            if n < 3:
                x_quant(n + 1, 0, x_turn(n + 1, 0, None))
            if 27 <= n < 35:
                x_quant(4 + (n - 27) // 2, (n - 27) % 2, x_turn(4 + (n - 27) // 2, (n - 27) % 2, sorted_rows.pop(0)))
            cell_group(w, sc, 1, p_raw)
            if n < 3:
                x_quant(n + 1, 1, x_turn(n + 1, 1, None))
            if 26 <= n < 34:
                sorted_rows.append(x_sort(4 + (n - 26) // 2, (n - 26) % 2))
            cell_group(w, sc, 2, p_raw)
            cell_group(w, sc, 3, p_raw)
            waiting.append((h, w, scl, p_copy(p_raw)))
            if fresh is not None:
                w_quant(fresh[0], fresh[1], fresh[2])

        def score_group(name, a_which, a_tok, b_which, b_tok):
            acc = acc_bank(name)
            ah, ac = a_tok // 2048, a_tok % 2048
            bh, bc = b_tok // 2048, b_tok % 2048
            for g in range(4):
                nc.tensor.matmul_mx(
                    out=acc[:],
                    lhsT=pt_codes[(4 * a_which + g, ah)][:, ac : ac + P].bitcast(FP8X4),
                    lhsT_scale=pt_scales[(a_which, ah)][4 * g : P, ac : ac + P],
                    rhs=pt_codes[(4 * b_which + g, bh)][:, bc : bc + 512].bitcast(FP8X4),
                    rhs_scale=pt_scales[(b_which, bh)][4 * g : P, bc : bc + 512],
                    start=(g == 0),
                    stop=(g == 3),
                )
            return acc

        def mirror(ib, jb, o_all, fine):
            e_all = block_tile("e_all", [P, 4, 512], F32)
            for j in range(4):
                bank = psum.tile([P, 4, P], F32, name="o_bank", tag="turned", bufs=4)
                for i in range(4):
                    nc.tensor.transpose(bank[:, i, :], o_all[:, i, P * j : P * (j + 1)], ident[:])
                flat = bank[:].rearrange("p i q -> p (i q)")
                if ib == jb:
                    nc.vector.tensor_tensor(out=e_all[:, j, :], in0=flat, in1=o_all[:, j, :], op=ALU.add)
                else:
                    nc.vector.tensor_copy(out=e_all[:, j, :], in_=flat)
                if fine:
                    r0 = 512 * jb + P * j
                    nc.sync.dma_start(out=out_rows[r0 : r0 + P, 512 * ib : 512 * (ib + 1)], in_=e_all[:, j, :])
            if not fine:
                nc.sync.dma_start(
                    out=out_rows[512 * jb : 512 * (jb + 1), 512 * ib : 512 * (ib + 1)].rearrange(
                        "(j p) c -> p j c", p=P
                    ),
                    in_=e_all[:],
                )

        owed = []
        for jb in range(8):
            for ib in range(jb + 1):
                o_all = block_tile("o_all", [P, 4, 512], F32)
                passes = 0
                for i in range(4):
                    tok = 512 * ib + P * i
                    acc_a = score_group("acc_a", 0, tok, 1, 512 * jb)
                    passes += 4
                    if ib == jb:
                        nc.scalar.activation(out=o_all[:, i, :], in_=acc_a[:], func=ACT.Relu, scale=OUT_SCALE)
                    else:
                        acc_b = score_group("acc_b", 1, tok, 0, 512 * jb)
                        passes += 4
                        half = small_tile("half", [P, 512], F32)
                        nc.scalar.activation(out=half[:], in_=acc_a[:], func=ACT.Relu, scale=OUT_SCALE)
                        nc.scalar.activation(out=o_all[:, i, :], in_=acc_b[:], func=ACT.Relu, scale=OUT_SCALE)
                        nc.vector.tensor_tensor(out=o_all[:, i, :], in0=o_all[:, i, :], in1=half[:], op=ALU.add)
                    if waiting:
                        qh, qw, qscl, qg = waiting.pop(0)
                        p_quant(qh, qw, qscl, qg)
                    if owed and passes >= 8:
                        oi, oj, oo = owed.pop(0)
                        mirror(oi, oj, oo, False)
                if ib != jb:
                    nc.sync.dma_start(
                        out=out_rows[512 * ib : 512 * (ib + 1), 512 * jb : 512 * (jb + 1)].rearrange(
                            "(i p) c -> p i c", p=P
                        ),
                        in_=o_all[:],
                    )
                owed.append((ib, jb, o_all))
        oi, oj, oo = owed.pop(0)
        mirror(oi, oj, oo, True)
